import numpy as np
import ml_dtypes


def mxq(x, axis, fmt="e4m3"):
    dtype, down = {"e4m3": (ml_dtypes.float8_e4m3fn, 7), "e5m2": (ml_dtypes.float8_e5m2, 14)}[fmt]
    v = np.moveaxis(np.asarray(x, np.float32).astype(ml_dtypes.bfloat16).astype(np.float64), axis, -1)
    blocks = v.reshape(v.shape[:-1] + (-1, 32))
    amax = np.abs(blocks).max(-1, keepdims=True)
    byte = np.maximum(np.where(amax > 0, np.frexp(amax)[1] - 1 + 127, 0) - down, 1)
    scale = np.exp2(byte - 127.0)
    codes = (blocks / scale).astype(np.float32).astype(dtype).astype(np.float64)
    return np.moveaxis((codes * scale).reshape(v.shape), -1, axis)


WIDE = False


def mx_kscale(k):
    if not WIDE:
        return np.ones(k)
    levels = np.array([10, -10, 5, -5, 0])
    a = np.random.permutation(np.resize(levels, k // 512 * 4)).reshape(k // 512, 4)
    idx = np.arange(k)
    return np.exp2(a[idx // 512, idx % 128 // 32])


BF16 = ml_dtypes.bfloat16


def bf(x):
    return np.asarray(x, np.float32).astype(BF16)


def f64(x):
    return np.asarray(x).astype(np.float64)


E2M1 = np.array([0.0, 0.5, 1.0, 1.5, 2.0, 3.0, 4.0, 6.0, -0.0, -0.5, -1.0, -1.5, -2.0, -3.0, -4.0, -6.0])


def pack_weight(w, fmt):
    k, n = w.shape
    w = f64(bf(w)).reshape(k // 32, 32, n)
    amax = np.abs(w).max(1)
    if fmt == "e4m3":
        byte = np.frexp(amax)[1] - 1 + 127 - 7
    else:
        mant, ex = np.frexp(amax / 6.0)
        byte = np.where(mant > 0.5, ex, ex - 1) + 127
    byte = np.clip(np.where(amax > 0, byte, 1), 1, 254)
    scaled = (w * np.exp2(127.0 - byte)[:, None, :]).reshape(k, n).astype(np.float32)
    by_word = np.ascontiguousarray(scaled.reshape(k // 512, 128, 4, n).transpose(0, 1, 3, 2))
    if fmt == "e4m3":
        words = by_word.astype(ml_dtypes.float8_e4m3fn).view(np.uint8)
    else:
        c = by_word.astype(ml_dtypes.float4_e2m1fn).view(np.uint8) & 0xF
        words = c[..., 0::2] | (c[..., 1::2] << 4)
    return np.ascontiguousarray(words), np.ascontiguousarray(byte.astype(np.uint8).reshape(k // 512, 16, n))


def unpack_weight(words, scales, fmt):
    g, p, n, _ = words.shape
    if fmt == "e4m3":
        vals = np.ascontiguousarray(words).view(ml_dtypes.float8_e4m3fn).astype(np.float64)
    else:
        nib = np.empty((g, p, n, 4), np.uint8)
        nib[..., 0::2] = words & 0xF
        nib[..., 1::2] = words >> 4
        vals = E2M1[nib]
    vals = vals * np.repeat(np.exp2(scales.astype(np.float64) - 127.0), 8, axis=1)[..., None]
    return vals.transpose(0, 1, 3, 2).reshape(g * 512, n)


B, S, D, H, DK, DV, C = 1, 128, 8192, 16, 128, 128, 512
THETA = 10000.0
SCALE_BASE = 512.0
FMT = "e4m3"


def rotate_half(t):
    tr = t.reshape(t.shape[:-1] + (-1, 2))
    return np.stack((-tr[..., 1], tr[..., 0]), axis=-1).reshape(t.shape)


def xpos_tables():
    pos = np.arange(S, dtype=np.float64)
    even = np.arange(0, DK, 2, dtype=np.float64)
    inv_freq = 1.0 / THETA ** (even / DK)
    freqs = np.repeat(pos[:, None] * inv_freq[None, :], 2, axis=-1)
    sbase = (even + 0.4 * DK) / (1.4 * DK)
    power = (pos - S // 2) / SCALE_BASE
    scale = np.repeat(sbase[None, :] ** power[:, None], 2, axis=-1)
    return np.cos(freqs), np.sin(freqs), scale


def heads(t):
    return t.reshape(B, S, H, -1).transpose(0, 2, 1, 3)


def setup_inputs():
    s = mx_kscale(D)
    x = bf(np.random.standard_normal((B, S, D)) * s)
    Wq_words, Wq_scales = pack_weight(np.random.standard_normal((D, H * DK)) * 0.25 / np.sqrt(D) / s[:, None], FMT)
    bq = bf(np.random.standard_normal(H * DK) * 0.1)
    Wk_words, Wk_scales = pack_weight(np.random.standard_normal((D, H * DK)) * 0.25 / np.sqrt(D) / s[:, None], FMT)
    bk = bf(np.random.standard_normal(H * DK) * 0.1)
    return {"x": x,
            "Wq_words": Wq_words,
            "Wq_scales": Wq_scales,
            "bq": bq,
            "Wk_words": Wk_words,
            "Wk_scales": Wk_scales,
            "bk": bk}


def reference(x, Wq_words, Wq_scales, bq, Wk_words, Wk_scales, bk):
    xq = mxq(f64(x), 2, "e4m3")
    q = heads((xq @ unpack_weight(Wq_words, Wq_scales, FMT)) + f64(bq))
    k = heads((xq @ unpack_weight(Wk_words, Wk_scales, FMT)) + f64(bk))
    cos, sin, scale = xpos_tables()
    q_rot = (q * cos + rotate_half(q) * sin) * scale
    k_rot = (k * cos + rotate_half(k) * sin) / scale
    return q_rot, k_rot

@@ -1,0 +1,294 @@
+import math
+
+import concourse.mybir as mybir
+from concourse.masks import make_identity
+
+F32 = mybir.dt.float32
+BF16 = mybir.dt.bfloat16
+I32 = mybir.dt.int32
+U32 = mybir.dt.uint32
+U8 = mybir.dt.uint8
+FP8X4 = mybir.dt.float8_e4m3fn_x4
+ALU = mybir.AluOpType
+ACT = mybir.ActivationFunctionType
+
+P = 128
+D = 8192
+PACK = 4
+K_PASS = P * PACK
+GROUPS = D // K_PASS
+HEADS = 16
+FEATURES = 128
+PAIRS = FEATURES // 2
+N_OUT = HEADS * FEATURES
+N_BANK = 512
+BANKS = N_OUT // N_BANK
+BANK_HEADS = N_BANK // FEATURES
+BANK_PAIRS = N_BANK // 2
+
+PLANES = 4
+QUADRANTS = 4
+QUADRANT = 32
+
+X_CHUNKS = 4
+CHUNK_GROUPS = GROUPS // X_CHUNKS
+BANK_GROUPS = 2
+
+TAIL_GROUPS = 4
+WEIGHT_BUFS = 12
+
+THETA = 10000.0
+SCALE_BASE = 512.0
+
+FLOPS = 2 * P * D * 2 * N_OUT
+
+
+def rotation_tables(nc, const, scratch):
+    pos_i = scratch.tile([P, 1], I32)
+    nc.gpsimd.iota(pos_i[:], pattern=[[0, 1]], base=0, channel_multiplier=1)
+    pair_i = scratch.tile([P, PAIRS], I32)
+    nc.gpsimd.iota(pair_i[:], pattern=[[1, PAIRS]], base=0, channel_multiplier=0)
+    pos = scratch.tile([P, 1], F32)
+    nc.vector.tensor_copy(out=pos[:], in_=pos_i[:])
+    pair = scratch.tile([P, PAIRS], F32)
+    nc.vector.tensor_copy(out=pair[:], in_=pair_i[:])
+
+    base = scratch.tile([P, PAIRS], F32)
+    nc.vector.tensor_scalar(
+        out=base[:],
+        in0=pair[:],
+        scalar1=2.0 / (1.4 * FEATURES),
+        scalar2=0.4 / 1.4,
+        op0=ALU.mult,
+        op1=ALU.add,
+    )
+    power = scratch.tile([P, 1], F32)
+    nc.vector.tensor_scalar(
+        out=power[:],
+        in0=pos[:],
+        scalar1=-float(P // 2),
+        scalar2=1.0 / SCALE_BASE,
+        op0=ALU.add,
+        op1=ALU.mult,
+    )
+    ln_base = scratch.tile([P, PAIRS], F32)
+    nc.scalar.activation(out=ln_base[:], in_=base[:], func=ACT.Ln)
+    exponent = scratch.tile([P, 2, PAIRS], F32)
+    nc.vector.tensor_scalar_mul(out=exponent[:, 0, :], in0=ln_base[:], scalar1=power[:, 0:1])
+    nc.vector.tensor_scalar_mul(out=exponent[:, 1, :], in0=exponent[:, 0, :], scalar1=-1.0)
+
+    freq = scratch.tile([P, PAIRS], F32)
+    nc.scalar.activation(out=freq[:], in_=pair[:], func=ACT.Exp, scale=-math.log(THETA) / PAIRS)
+    xpos_scale = scratch.tile([P, 2, PAIRS], F32)
+    nc.scalar.activation(out=xpos_scale[:], in_=exponent[:], func=ACT.Exp)
+
+    turns = scratch.tile([P, 2, PAIRS], F32)
+    nc.vector.tensor_scalar(
+        out=turns[:, 1, :],
+        in0=freq[:],
+        scalar1=pos[:, 0:1],
+        scalar2=1.0 / (2.0 * math.pi),
+        op0=ALU.mult,
+        op1=ALU.mult,
+    )
+    nc.vector.tensor_scalar_add(out=turns[:, 0, :], in0=turns[:, 1, :], scalar1=0.25)
+
+    whole_i = scratch.tile([P, 2, PAIRS], I32)
+    nc.vector.tensor_copy(out=whole_i[:], in_=turns[:])
+    whole = scratch.tile([P, 2, PAIRS], F32)
+    nc.vector.tensor_copy(out=whole[:], in_=whole_i[:])
+    part = scratch.tile([P, 2, PAIRS], F32)
+    nc.vector.tensor_tensor(out=part[:], in0=turns[:], in1=whole[:], op=ALU.subtract)
+    above = scratch.tile([P, 2, PAIRS], F32)
+    nc.vector.tensor_single_scalar(out=above[:], in_=part[:], scalar=0.5, op=ALU.is_gt)
+    wrapped = scratch.tile([P, 2, PAIRS], F32)
+    nc.vector.tensor_tensor(out=wrapped[:], in0=part[:], in1=above[:], op=ALU.subtract)
+    cos_sin = scratch.tile([P, 2, PAIRS], F32)
+    nc.scalar.activation(out=cos_sin[:], in_=wrapped[:], func=ACT.Sin, scale=2.0 * math.pi)
+
+    rot = const.tile([P, 2, 2, PAIRS], F32)
+    for w in range(2):
+        nc.vector.tensor_tensor(
+            out=rot[:, w, :, :],
+            in0=cos_sin[:],
+            in1=xpos_scale[:, w, :].unsqueeze(1).to_broadcast([P, 2, PAIRS]),
+            op=ALU.mult,
+        )
+    return rot
+
+
+def rotate_bank(nc, work, bank, cos_sin):
+    shape = [P, 2, BANK_HEADS, PAIRS]
+    halves = bank.rearrange("p (h m e) -> p e h m", h=BANK_HEADS, e=2)
+    by_cos = work.tile(shape, F32)
+    nc.vector.tensor_tensor(
+        out=by_cos[:],
+        in0=halves,
+        in1=cos_sin[:, 0, :].unsqueeze(1).unsqueeze(1).to_broadcast(shape),
+        op=ALU.mult,
+    )
+    by_sin = work.tile(shape, F32)
+    nc.vector.tensor_tensor(
+        out=by_sin[:],
+        in0=halves,
+        in1=cos_sin[:, 1, :].unsqueeze(1).unsqueeze(1).to_broadcast(shape),
+        op=ALU.mult,
+    )
+    rotated = work.tile(shape, F32)
+    nc.vector.tensor_tensor(
+        out=rotated[:, 0], in0=by_cos[:, 0], in1=by_sin[:, 1], op=ALU.subtract
+    )
+    nc.vector.tensor_tensor(out=rotated[:, 1], in0=by_cos[:, 1], in1=by_sin[:, 0], op=ALU.add)
+    return rotated
+
+
+def tile_gatedmultiscaleretentionlayer_pa_k_kernel(
+    tc, x, Wq_words, Wq_scales, bq, Wk_words, Wk_scales, bk, out_0, out_1
+):
+    nc = tc.nc
+    with (
+        tc.manual_schedule(),
+        tc.tile_pool(name="const", bufs=1) as const,
+        tc.tile_pool(name="scratch", bufs=1) as scratch,
+        tc.tile_pool(name="weights", bufs=WEIGHT_BUFS) as weights,
+        tc.tile_pool(name="work", bufs=2) as work,
+        tc.psum_pool(name="psum", bufs=8) as psum,
+    ):
+        bias_rows = const.tile([P, 2, N_OUT], BF16)
+        nc.vector.memset(bias_rows[:].bitcast(I32), 0)
+        ones = const.tile([P, P], BF16)
+        nc.vector.memset(ones[:], 1.0)
+        w_planes = const.tile([P, 2, GROUPS // PLANES, N_OUT], U8, align_bytes=64)
+        nc.vector.memset(w_planes[:].bitcast(I32), 0)
+
+        x_sb = const.tile([P, D], BF16)
+        chunk_cols = D // X_CHUNKS
+        for c in range(X_CHUNKS):
+            cols = slice(c * chunk_cols, (c + 1) * chunk_cols)
+            nc.sync.dma_start(out=x_sb[:, cols], in_=x[0, :, cols])
+        for w, bias in enumerate((bq, bk)):
+            nc.sync.dma_start(out=bias_rows[0:1, w, :], in_=bias.unsqueeze(0))
+        for w, scales in enumerate((Wq_scales, Wk_scales)):
+            for a in range(GROUPS // PLANES):
+                for quadrant in range(QUADRANTS):
+                    first = QUADRANT * quadrant
+                    nc.sync.dma_start(
+                        out=w_planes[first : first + PLANES * 4, w, a, :].bitcast(I32),
+                        in_=scales[
+                            PLANES * a : PLANES * (a + 1), 4 * quadrant : 4 * (quadrant + 1), :
+                        ].bitcast(I32),
+                    )
+
+        rot = rotation_tables(nc, const, scratch)
+        ident = const.tile([P, P], F32)
+        make_identity(nc, ident[:])
+
+        x_words = x_sb[:].bitcast(F32)
+        group_words = K_PASS // 2
+        grouped = const.tile([P, GROUPS, P, PACK], BF16, align_bytes=64)
+        grouped_words = grouped[:].bitcast(F32)
+        x_codes = const.tile([P, GROUPS, P], U32, align_bytes=64)
+        x_planes = const.tile([P, GROUPS, P], U8, align_bytes=64)
+        for c in range(X_CHUNKS):
+            for half in range(CHUNK_GROUPS // BANK_GROUPS):
+                g0 = c * CHUNK_GROUPS + half * BANK_GROUPS
+                xt = psum.tile([P, BANK_GROUPS, 2, P], F32, tag="bank")
+                for i in range(BANK_GROUPS):
+                    for u in range(2):
+                        first = (g0 + i) * group_words + u
+                        nc.tensor.transpose(
+                            out=xt[:, i, u, :],
+                            in_=x_words[:, first : (g0 + i + 1) * group_words : 2],
+                            identity=ident[:],
+                        )
+                copy = nc.vector.tensor_copy if half % 2 == 0 else nc.scalar.copy
+                copy(
+                    out=grouped_words[:, g0 : g0 + BANK_GROUPS, :, :],
+                    in_=xt[:].rearrange("p g u r -> p g r u"),
+                )
+            gs = slice(c * CHUNK_GROUPS, (c + 1) * CHUNK_GROUPS)
+            nc.vector.quantize_mx(
+                out=x_codes[:, gs, :].rearrange("p g r -> p (g r)").bitcast(FP8X4),
+                scales=x_planes[:, gs, :].rearrange("p g r -> p (g r)"),
+                in_=grouped[:, gs, :, :].rearrange("p g r t -> p (g r t)"),
+            )
+
+        bias_rot = const.tile([P, 2, N_OUT], F32)
+        for w in range(2):
+            for j in range(BANKS):
+                cols = slice(j * N_BANK, (j + 1) * N_BANK)
+                spread = psum.tile([P, N_BANK], F32, tag="bank")
+                nc.tensor.matmul(
+                    out=spread[:], lhsT=ones[:], rhs=bias_rows[:, w, cols], start=True, stop=True
+                )
+                rotated = rotate_bank(nc, work, spread[:], rot[:, w])
+                nc.vector.tensor_copy(
+                    out=bias_rot[:, w, cols].rearrange(
+                        "p (h m e) -> p h m e", h=BANK_HEADS, e=2
+                    ),
+                    in_=rotated[:].rearrange("p e h m -> p h m e"),
+                )
+
+        def multiply(acc, g, w, j, words, start, stop):
+            offset = 4 * (g % PLANES)
+            nc.tensor.matmul_mx(
+                out=acc[:],
+                lhsT=x_codes[:, g, :].bitcast(FP8X4),
+                lhsT_scale=x_planes[:, g, :],
+                rhs=words.bitcast(FP8X4),
+                rhs_scale=w_planes[offset:P, w, g // PLANES, j * N_BANK : (j + 1) * N_BANK],
+                start=start,
+                stop=stop,
+            )
+
+        def finish(acc, w, j, out, queue):
+            rotated = rotate_bank(nc, work, acc[:], rot[:, w])
+            result = work.tile([P, BANK_HEADS, PAIRS, 2], F32)
+            nc.vector.tensor_tensor(
+                out=result[:],
+                in0=rotated[:].rearrange("p e h m -> p h m e"),
+                in1=bias_rot[:, w, j * N_BANK : (j + 1) * N_BANK].rearrange(
+                    "p (h m e) -> p h m e", h=BANK_HEADS, e=2
+                ),
+                op=ALU.add,
+            )
+            queue.dma_start(
+                out=out[0, j * BANK_HEADS : (j + 1) * BANK_HEADS].rearrange("h p f -> p h f"),
+                in_=result[:].rearrange("p h m e -> p h (m e)"),
+            )
+
+        def load_group(words_dram, g):
+            tile = weights.tile([P, BANKS, N_BANK], U32, tag="words", align_bytes=64)
+            nc.sync.dma_start(
+                out=tile[:].rearrange("p j n -> p (j n)").bitcast(I32),
+                in_=words_dram[g].rearrange("p n t -> p (n t)").bitcast(I32),
+            )
+            return tile
+
+        q_acc = [psum.tile([P, N_BANK], F32, tag="bank", name="q_acc%d" % j) for j in range(BANKS)]
+        for g in range(GROUPS):
+            tile = load_group(Wq_words, g)
+            for j in range(BANKS):
+                multiply(q_acc[j], g, 0, j, tile[:, j, :], g == 0, g == GROUPS - 1)
+        for j in range(BANKS):
+            finish(q_acc[j], 0, j, out_0, nc.scalar)
+
+        k_acc = [psum.tile([P, N_BANK], F32, tag="bank", name="k_acc%d" % j) for j in range(BANKS)]
+        body = GROUPS - TAIL_GROUPS
+        for g in range(body):
+            tile = load_group(Wk_words, g)
+            for j in range(BANKS):
+                multiply(k_acc[j], g, 1, j, tile[:, j, :], g == 0, False)
+        tail_dram = Wk_words[body:GROUPS].rearrange("g p n t -> p g (n t)")
+        tail_tiles = []
+        for j in range(BANKS):
+            tile = weights.tile([P, TAIL_GROUPS, N_BANK], U32, tag="words", align_bytes=64)
+            nc.sync.dma_start(
+                out=tile[:].bitcast(I32),
+                in_=tail_dram[:, :, j * N_BANK * PACK : (j + 1) * N_BANK * PACK].bitcast(I32),
+            )
+            tail_tiles.append(tile)
+        for j in range(BANKS):
+            for i in range(TAIL_GROUPS):
+                multiply(k_acc[j], body + i, 1, j, tail_tiles[j][:, i, :], False, i == TAIL_GROUPS - 1)
+            finish(k_acc[j], 1, j, out_1, nc.sync)

@@ -156,10 +156,10 @@ def tile_gatedmultiscaleretentionlayer_pa_k_kernel(
     ):
         bias_rows = const.tile([P, 2, N_OUT], BF16)
         nc.vector.memset(bias_rows[:].bitcast(I32), 0)
-        ones = const.tile([P, P], BF16)
-        nc.vector.memset(ones[:], 1.0)
         w_planes = const.tile([P, 2, GROUPS // PLANES, N_OUT], U8, align_bytes=64)
         nc.vector.memset(w_planes[:].bitcast(I32), 0)
+        ones = const.tile([P, P], BF16)
+        nc.vector.memset(ones[:], 1.0)
 
         x_sb = const.tile([P, D], BF16)
         chunk_cols = D // X_CHUNKS
@@ -168,20 +168,21 @@ def tile_gatedmultiscaleretentionlayer_pa_k_kernel(
             nc.sync.dma_start(out=x_sb[:, cols], in_=x[0, :, cols])
         for w, bias in enumerate((bq, bk)):
             nc.sync.dma_start(out=bias_rows[0:1, w, :], in_=bias.unsqueeze(0))
-        for w, scales in enumerate((Wq_scales, Wk_scales)):
-            for a in range(GROUPS // PLANES):
-                for quadrant in range(QUADRANTS):
-                    first = QUADRANT * quadrant
-                    nc.sync.dma_start(
-                        out=w_planes[first : first + PLANES * 4, w, a, :].bitcast(I32),
-                        in_=scales[
-                            PLANES * a : PLANES * (a + 1), 4 * quadrant : 4 * (quadrant + 1), :
-                        ].bitcast(I32),
-                    )
 
         rot = rotation_tables(nc, const, scratch)
         ident = const.tile([P, P], F32)
         make_identity(nc, ident[:])
+
+        for w, scales in enumerate((Wq_scales, Wk_scales)):
+            for a in range(GROUPS // PLANES):
+                for quadrant in range(QUADRANTS):
+                    first = QUADRANT * quadrant
+                    nc.gpsimd.dma_start(
+                        out=w_planes[first : first + PLANES * 4, w, a, :].bitcast(F32),
+                        in_=scales[
+                            PLANES * a : PLANES * (a + 1), 4 * quadrant : 4 * (quadrant + 1), :
+                        ].bitcast(F32),
+                    )
 
         x_words = x_sb[:].bitcast(F32)
         group_words = K_PASS // 2

@@ -35,7 +35,7 @@ CHUNK_GROUPS = GROUPS // X_CHUNKS
 BANK_GROUPS = 2
 
 TAIL_GROUPS = 4
-WEIGHT_BUFS = 12
+WEIGHT_BUFS = 14
 
 THETA = 10000.0
 SCALE_BASE = 512.0
@@ -242,20 +242,15 @@ def tile_gatedmultiscaleretentionlayer_pa_k_kernel(
                 stop=stop,
             )
 
-        def finish(acc, w, j, out, queue):
+        def finish(acc, w, j, result):
             rotated = rotate_bank(nc, work, acc[:], rot[:, w])
-            result = work.tile([P, BANK_HEADS, PAIRS, 2], F32)
             nc.vector.tensor_tensor(
-                out=result[:],
+                out=result.rearrange("p (h m e) -> p h m e", h=BANK_HEADS, e=2),
                 in0=rotated[:].rearrange("p e h m -> p h m e"),
                 in1=bias_rot[:, w, j * N_BANK : (j + 1) * N_BANK].rearrange(
                     "p (h m e) -> p h m e", h=BANK_HEADS, e=2
                 ),
                 op=ALU.add,
-            )
-            queue.dma_start(
-                out=out[0, j * BANK_HEADS : (j + 1) * BANK_HEADS].rearrange("h p f -> p h f"),
-                in_=result[:].rearrange("p h m e -> p h (m e)"),
             )
 
         def load_group(words_dram, g):
@@ -271,8 +266,9 @@ def tile_gatedmultiscaleretentionlayer_pa_k_kernel(
             tile = load_group(Wq_words, g)
             for j in range(BANKS):
                 multiply(q_acc[j], g, 0, j, tile[:, j, :], g == 0, g == GROUPS - 1)
+        q_result = const.tile([P, BANKS, N_BANK], F32)
         for j in range(BANKS):
-            finish(q_acc[j], 0, j, out_0, nc.scalar)
+            finish(q_acc[j], 0, j, q_result[:, j, :])
 
         k_acc = [psum.tile([P, N_BANK], F32, tag="bank", name="k_acc%d" % j) for j in range(BANKS)]
         body = GROUPS - TAIL_GROUPS
@@ -280,16 +276,28 @@ def tile_gatedmultiscaleretentionlayer_pa_k_kernel(
             tile = load_group(Wk_words, g)
             for j in range(BANKS):
                 multiply(k_acc[j], g, 1, j, tile[:, j, :], g == 0, False)
-        tail_dram = Wk_words[body:GROUPS].rearrange("g p n t -> p g (n t)")
         tail_tiles = []
         for j in range(BANKS):
             tile = weights.tile([P, TAIL_GROUPS, N_BANK], U32, tag="words", align_bytes=64)
-            nc.sync.dma_start(
-                out=tile[:].bitcast(I32),
-                in_=tail_dram[:, :, j * N_BANK * PACK : (j + 1) * N_BANK * PACK].bitcast(I32),
-            )
+            for i in range(TAIL_GROUPS):
+                block = Wk_words[body + i].rearrange("p n t -> p (n t)")[
+                    :, j * N_BANK * PACK : (j + 1) * N_BANK * PACK
+                ]
+                nc.sync.dma_start(out=tile[:, i, :].bitcast(I32), in_=block.bitcast(I32))
             tail_tiles.append(tile)
+
+        nc.sync.dma_start(
+            out=out_0[0].rearrange("h p f -> p h f"),
+            in_=q_result[:].rearrange("p j (h f) -> p (j h) f", f=FEATURES),
+        )
         for j in range(BANKS):
             for i in range(TAIL_GROUPS):
-                multiply(k_acc[j], body + i, 1, j, tail_tiles[j][:, i, :], False, i == TAIL_GROUPS - 1)
-            finish(k_acc[j], 1, j, out_1, nc.sync)
+                multiply(
+                    k_acc[j], body + i, 1, j, tail_tiles[j][:, i, :], False, i == TAIL_GROUPS - 1
+                )
+            k_result = work.tile([P, N_BANK], F32)
+            finish(k_acc[j], 1, j, k_result[:])
+            nc.sync.dma_start(
+                out=out_1[0, j * BANK_HEADS : (j + 1) * BANK_HEADS].rearrange("h p f -> p h f"),
+                in_=k_result[:].rearrange("p (h f) -> p h f", f=FEATURES),
+            )

@@ -37,6 +37,8 @@ BANK_GROUPS = 2
 TAIL_GROUPS = 4
 WEIGHT_BUFS = 14
 
+FIRST_BIAS_GROUP = 3
+
 THETA = 10000.0
 SCALE_BASE = 512.0
 
@@ -152,12 +154,14 @@ def tile_gatedmultiscaleretentionlayer_pa_k_kernel(
         tc.tile_pool(name="scratch", bufs=1) as scratch,
         tc.tile_pool(name="weights", bufs=WEIGHT_BUFS) as weights,
         tc.tile_pool(name="work", bufs=2) as work,
-        tc.psum_pool(name="psum", bufs=8) as psum,
+        tc.psum_pool(name="psum", bufs=4) as psum,
     ):
         bias_rows = const.tile([P, 2, N_OUT], BF16)
         nc.vector.memset(bias_rows[:].bitcast(I32), 0)
         w_planes = const.tile([P, 2, GROUPS // PLANES, N_OUT], U8, align_bytes=64)
-        nc.vector.memset(w_planes[:].bitcast(I32), 0)
+        for w in range(2):
+            for a in range(GROUPS // PLANES):
+                nc.vector.memset(w_planes[:, w, a, :].bitcast(I32), 0)
         ones = const.tile([P, P], BF16)
         nc.vector.memset(ones[:], 1.0)
 
@@ -169,7 +173,6 @@ def tile_gatedmultiscaleretentionlayer_pa_k_kernel(
         for w, bias in enumerate((bq, bk)):
             nc.sync.dma_start(out=bias_rows[0:1, w, :], in_=bias.unsqueeze(0))
 
-        rot = rotation_tables(nc, const, scratch)
         ident = const.tile([P, P], F32)
         make_identity(nc, ident[:])
 
@@ -193,7 +196,7 @@ def tile_gatedmultiscaleretentionlayer_pa_k_kernel(
         for c in range(X_CHUNKS):
             for half in range(CHUNK_GROUPS // BANK_GROUPS):
                 g0 = c * CHUNK_GROUPS + half * BANK_GROUPS
-                xt = psum.tile([P, BANK_GROUPS, 2, P], F32, tag="bank")
+                xt = psum.tile([P, BANK_GROUPS, 2, P], F32, tag="x_bank")
                 for i in range(BANK_GROUPS):
                     for u in range(2):
                         first = (g0 + i) * group_words + u
@@ -214,21 +217,20 @@ def tile_gatedmultiscaleretentionlayer_pa_k_kernel(
                 in_=grouped[:, gs, :, :].rearrange("p g r t -> p (g r t)"),
             )
 
+        rot = rotation_tables(nc, const, scratch)
         bias_rot = const.tile([P, 2, N_OUT], F32)
-        for w in range(2):
-            for j in range(BANKS):
-                cols = slice(j * N_BANK, (j + 1) * N_BANK)
-                spread = psum.tile([P, N_BANK], F32, tag="bank")
-                nc.tensor.matmul(
-                    out=spread[:], lhsT=ones[:], rhs=bias_rows[:, w, cols], start=True, stop=True
-                )
-                rotated = rotate_bank(nc, work, spread[:], rot[:, w])
-                nc.vector.tensor_copy(
-                    out=bias_rot[:, w, cols].rearrange(
-                        "p (h m e) -> p h m e", h=BANK_HEADS, e=2
-                    ),
-                    in_=rotated[:].rearrange("p e h m -> p h m e"),
-                )
+
+        def rotate_bias(w, j):
+            cols = slice(j * N_BANK, (j + 1) * N_BANK)
+            spread = psum.tile([P, N_BANK], F32, tag="x_bank")
+            nc.tensor.matmul(
+                out=spread[:], lhsT=ones[:], rhs=bias_rows[:, w, cols], start=True, stop=True
+            )
+            rotated = rotate_bank(nc, work, spread[:], rot[:, w])
+            nc.vector.tensor_copy(
+                out=bias_rot[:, w, cols].rearrange("p (h m e) -> p h m e", h=BANK_HEADS, e=2),
+                in_=rotated[:].rearrange("p e h m -> p h m e"),
+            )
 
         def multiply(acc, g, w, j, words, start, stop):
             offset = 4 * (g % PLANES)
@@ -261,16 +263,19 @@ def tile_gatedmultiscaleretentionlayer_pa_k_kernel(
             )
             return tile
 
-        q_acc = [psum.tile([P, N_BANK], F32, tag="bank", name="q_acc%d" % j) for j in range(BANKS)]
+        q_acc = [psum.tile([P, N_BANK], F32, tag="q_bank", name="q_acc%d" % j) for j in range(BANKS)]
         for g in range(GROUPS):
             tile = load_group(Wq_words, g)
             for j in range(BANKS):
                 multiply(q_acc[j], g, 0, j, tile[:, j, :], g == 0, g == GROUPS - 1)
+            b = g - FIRST_BIAS_GROUP
+            if 0 <= b < 2 * BANKS:
+                rotate_bias(b // BANKS, b % BANKS)
         q_result = const.tile([P, BANKS, N_BANK], F32)
         for j in range(BANKS):
             finish(q_acc[j], 0, j, q_result[:, j, :])
 
-        k_acc = [psum.tile([P, N_BANK], F32, tag="bank", name="k_acc%d" % j) for j in range(BANKS)]
+        k_acc = [psum.tile([P, N_BANK], F32, tag="x_bank", name="k_acc%d" % j) for j in range(BANKS)]
         body = GROUPS - TAIL_GROUPS
         for g in range(body):
             tile = load_group(Wk_words, g)

@@ -35,9 +35,13 @@ CHUNK_GROUPS = GROUPS // X_CHUNKS
 BANK_GROUPS = 2
 
 TAIL_GROUPS = 4
-WEIGHT_BUFS = 14
+WEIGHT_BUFS = 12
 
 FIRST_BIAS_GROUP = 3
+
+RUNS = P // HEADS
+RUN = P // RUNS
+FIRST_TURN_GROUP = 2
 
 THETA = 10000.0
 SCALE_BASE = 512.0
@@ -45,11 +49,15 @@ SCALE_BASE = 512.0
 FLOPS = 2 * P * D * 2 * N_OUT
 
 
-def rotation_tables(nc, const, scratch):
+def index_tiles(nc, scratch):
     pos_i = scratch.tile([P, 1], I32)
     nc.gpsimd.iota(pos_i[:], pattern=[[0, 1]], base=0, channel_multiplier=1)
     pair_i = scratch.tile([P, PAIRS], I32)
     nc.gpsimd.iota(pair_i[:], pattern=[[1, PAIRS]], base=0, channel_multiplier=0)
+    return pos_i, pair_i
+
+
+def rotation_tables(nc, const, scratch, pos_i, pair_i):
     pos = scratch.tile([P, 1], F32)
     nc.vector.tensor_copy(out=pos[:], in_=pos_i[:])
     pair = scratch.tile([P, PAIRS], F32)
@@ -175,6 +183,7 @@ def tile_gatedmultiscaleretentionlayer_pa_k_kernel(
 
         ident = const.tile([P, P], F32)
         make_identity(nc, ident[:])
+        pos_i, pair_i = index_tiles(nc, scratch)
 
         for w, scales in enumerate((Wq_scales, Wk_scales)):
             for a in range(GROUPS // PLANES):
@@ -217,7 +226,7 @@ def tile_gatedmultiscaleretentionlayer_pa_k_kernel(
                 in_=grouped[:, gs, :, :].rearrange("p g r t -> p (g r t)"),
             )
 
-        rot = rotation_tables(nc, const, scratch)
+        rot = rotation_tables(nc, const, scratch, pos_i, pair_i)
         bias_rot = const.tile([P, 2, N_OUT], F32)
 
         def rotate_bias(w, j):
@@ -275,12 +284,41 @@ def tile_gatedmultiscaleretentionlayer_pa_k_kernel(
         for j in range(BANKS):
             finish(q_acc[j], 0, j, q_result[:, j, :])
 
+        q_turned = const.tile([P, RUN, HEADS, RUNS], F32)
+        q_out = const.tile([P, RUN, FEATURES], F32)
+
+        def turn_heads(j):
+            turned = psum.tile([P, BANK_HEADS, P], F32, tag="q_bank")
+            for i in range(BANK_HEADS):
+                cols = slice(i * FEATURES, (i + 1) * FEATURES)
+                nc.tensor.transpose(
+                    out=turned[:, i, :], in_=q_result[:, j, cols], identity=ident[:]
+                )
+            nc.scalar.copy(
+                out=q_turned[:, :, j * BANK_HEADS : (j + 1) * BANK_HEADS, :],
+                in_=turned[:].rearrange("f h (b r) -> f r h b", r=RUN),
+            )
+
+        def turn_runs(r0):
+            turned = psum.tile([P, BANK_HEADS, FEATURES], F32, tag="q_bank")
+            for i in range(BANK_HEADS):
+                nc.tensor.transpose(
+                    out=turned[:, i, :],
+                    in_=q_turned[:, r0 + i, :, :].rearrange("f h b -> f (h b)"),
+                    identity=ident[:],
+                )
+            nc.scalar.copy(out=q_out[:, r0 : r0 + BANK_HEADS, :], in_=turned[:])
+
         k_acc = [psum.tile([P, N_BANK], F32, tag="x_bank", name="k_acc%d" % j) for j in range(BANKS)]
         body = GROUPS - TAIL_GROUPS
         for g in range(body):
             tile = load_group(Wk_words, g)
             for j in range(BANKS):
                 multiply(k_acc[j], g, 1, j, tile[:, j, :], g == 0, False)
+            if FIRST_TURN_GROUP <= g < FIRST_TURN_GROUP + BANKS:
+                turn_heads(g - FIRST_TURN_GROUP)
+            if FIRST_TURN_GROUP + BANKS <= g < FIRST_TURN_GROUP + 2 * BANKS:
+                turn_runs((g - FIRST_TURN_GROUP - BANKS) * BANK_HEADS)
         tail_tiles = []
         for j in range(BANKS):
             tile = weights.tile([P, TAIL_GROUPS, N_BANK], U32, tag="words", align_bytes=64)
@@ -292,8 +330,8 @@ def tile_gatedmultiscaleretentionlayer_pa_k_kernel(
             tail_tiles.append(tile)
 
         nc.sync.dma_start(
-            out=out_0[0].rearrange("h p f -> p h f"),
-            in_=q_result[:].rearrange("p j (h f) -> p (j h) f", f=FEATURES),
+            out=out_0[0].rearrange("h (b r) f -> (h b) (r f)", r=RUN),
+            in_=q_out[:].rearrange("p r f -> p (r f)"),
         )
         for j in range(BANKS):
             for i in range(TAIL_GROUPS):

@@ -333,14 +333,14 @@ def tile_gatedmultiscaleretentionlayer_pa_k_kernel(
             out=out_0[0].rearrange("h (b r) f -> (h b) (r f)", r=RUN),
             in_=q_out[:].rearrange("p r f -> p (r f)"),
         )
+        k_result = const.tile([P, BANKS, N_BANK], F32)
         for j in range(BANKS):
             for i in range(TAIL_GROUPS):
                 multiply(
                     k_acc[j], body + i, 1, j, tail_tiles[j][:, i, :], False, i == TAIL_GROUPS - 1
                 )
-            k_result = work.tile([P, N_BANK], F32)
-            finish(k_acc[j], 1, j, k_result[:])
+            finish(k_acc[j], 1, j, k_result[:, j, :])
             nc.sync.dma_start(
                 out=out_1[0, j * BANK_HEADS : (j + 1) * BANK_HEADS].rearrange("h p f -> p h f"),
-                in_=k_result[:].rearrange("p (h f) -> p h f", f=FEATURES),
+                in_=k_result[:, j, :].rearrange("p (h f) -> p h f", f=FEATURES),
             )

@@ -34,14 +34,27 @@ X_CHUNKS = 4
 CHUNK_GROUPS = GROUPS // X_CHUNKS
 BANK_GROUPS = 2
 
-TAIL_GROUPS = 4
+K_BLOCKS = ((0, 512), (512, 512), (1024, 512), (1536, 256), (1792, 256))
+BODY_GROUPS = 8
+TAIL_LOADS = (
+    (8, 2, 0, 1024),
+    (10, 2, 0, 1024),
+    (12, 2, 0, 1024),
+    (14, 2, 0, 1024),
+    (8, 2, 1024, 1024),
+    (10, 3, 1024, 512),
+    (13, 3, 1024, 512),
+    (10, 2, 1536, 512),
+    (12, 4, 1536, 256),
+    (12, 4, 1792, 256),
+)
 WEIGHT_BUFS = 12
 
 FIRST_BIAS_GROUP = 3
 
 RUNS = P // HEADS
 RUN = P // RUNS
-FIRST_TURN_GROUP = 2
+FIRST_TURN_GROUP = 3
 
 THETA = 10000.0
 SCALE_BASE = 512.0
@@ -128,8 +141,9 @@ def rotation_tables(nc, const, scratch, pos_i, pair_i):
 
 
 def rotate_bank(nc, work, bank, cos_sin):
-    shape = [P, 2, BANK_HEADS, PAIRS]
-    halves = bank.rearrange("p (h m e) -> p e h m", h=BANK_HEADS, e=2)
+    heads = bank.shape[1] // FEATURES
+    shape = [P, 2, heads, PAIRS]
+    halves = bank.rearrange("p (h m e) -> p e h m", h=heads, e=2)
     by_cos = work.tile(shape, F32)
     nc.vector.tensor_tensor(
         out=by_cos[:],
@@ -241,25 +255,26 @@ def tile_gatedmultiscaleretentionlayer_pa_k_kernel(
                 in_=rotated[:].rearrange("p e h m -> p h m e"),
             )
 
-        def multiply(acc, g, w, j, words, start, stop):
+        def multiply(acc, g, w, col, words, start, stop):
             offset = 4 * (g % PLANES)
             nc.tensor.matmul_mx(
                 out=acc[:],
                 lhsT=x_codes[:, g, :].bitcast(FP8X4),
                 lhsT_scale=x_planes[:, g, :],
                 rhs=words.bitcast(FP8X4),
-                rhs_scale=w_planes[offset:P, w, g // PLANES, j * N_BANK : (j + 1) * N_BANK],
+                rhs_scale=w_planes[offset:P, w, g // PLANES, col : col + words.shape[1]],
                 start=start,
                 stop=stop,
             )
 
-        def finish(acc, w, j, result):
+        def finish(acc, w, col, result):
+            width = result.shape[1]
             rotated = rotate_bank(nc, work, acc[:], rot[:, w])
             nc.vector.tensor_tensor(
-                out=result.rearrange("p (h m e) -> p h m e", h=BANK_HEADS, e=2),
+                out=result.rearrange("p (h m e) -> p h m e", m=PAIRS, e=2),
                 in0=rotated[:].rearrange("p e h m -> p h m e"),
-                in1=bias_rot[:, w, j * N_BANK : (j + 1) * N_BANK].rearrange(
-                    "p (h m e) -> p h m e", h=BANK_HEADS, e=2
+                in1=bias_rot[:, w, col : col + width].rearrange(
+                    "p (h m e) -> p h m e", m=PAIRS, e=2
                 ),
                 op=ALU.add,
             )
@@ -272,23 +287,26 @@ def tile_gatedmultiscaleretentionlayer_pa_k_kernel(
             )
             return tile
 
-        q_acc = [psum.tile([P, N_BANK], F32, tag="q_bank", name="q_acc%d" % j) for j in range(BANKS)]
+        q_acc = []
+        for j in range(BANKS):
+            tag, bufs = ("last_bank", 1) if j == 0 else ("q_bank", 3)
+            q_acc.append(psum.tile([P, N_BANK], F32, tag=tag, bufs=bufs, name="q_acc%d" % j))
         for g in range(GROUPS):
             tile = load_group(Wq_words, g)
             for j in range(BANKS):
-                multiply(q_acc[j], g, 0, j, tile[:, j, :], g == 0, g == GROUPS - 1)
+                multiply(q_acc[j], g, 0, j * N_BANK, tile[:, j, :], g == 0, g == GROUPS - 1)
             b = g - FIRST_BIAS_GROUP
             if 0 <= b < 2 * BANKS:
                 rotate_bias(b // BANKS, b % BANKS)
         q_result = const.tile([P, BANKS, N_BANK], F32)
         for j in range(BANKS):
-            finish(q_acc[j], 0, j, q_result[:, j, :])
+            finish(q_acc[j], 0, j * N_BANK, q_result[:, j, :])
 
         q_turned = const.tile([P, RUN, HEADS, RUNS], F32)
         q_out = const.tile([P, RUN, FEATURES], F32)
 
         def turn_heads(j):
-            turned = psum.tile([P, BANK_HEADS, P], F32, tag="q_bank")
+            turned = psum.tile([P, BANK_HEADS, P], F32, tag="q_bank", bufs=3)
             for i in range(BANK_HEADS):
                 cols = slice(i * FEATURES, (i + 1) * FEATURES)
                 nc.tensor.transpose(
@@ -300,7 +318,7 @@ def tile_gatedmultiscaleretentionlayer_pa_k_kernel(
             )
 
         def turn_runs(r0):
-            turned = psum.tile([P, BANK_HEADS, FEATURES], F32, tag="q_bank")
+            turned = psum.tile([P, BANK_HEADS, FEATURES], F32, tag="q_bank", bufs=3)
             for i in range(BANK_HEADS):
                 nc.tensor.transpose(
                     out=turned[:, i, :],
@@ -309,38 +327,52 @@ def tile_gatedmultiscaleretentionlayer_pa_k_kernel(
                 )
             nc.scalar.copy(out=q_out[:, r0 : r0 + BANK_HEADS, :], in_=turned[:])
 
-        k_acc = [psum.tile([P, N_BANK], F32, tag="x_bank", name="k_acc%d" % j) for j in range(BANKS)]
-        body = GROUPS - TAIL_GROUPS
-        for g in range(body):
+        k_acc = {}
+
+        def multiply_k(g, first, cols, words):
+            for col, width in K_BLOCKS:
+                if first <= col < first + cols:
+                    if col not in k_acc:
+                        tag, bufs = ("x_bank", 4) if len(k_acc) < 4 else ("last_bank", 1)
+                        k_acc[col] = psum.tile(
+                            [P, width], F32, tag=tag, bufs=bufs, name="k_acc%d" % col
+                        )
+                    block = words[:, col - first : col - first + width]
+                    multiply(k_acc[col], g, 1, col, block, g == 0, g == GROUPS - 1)
+
+        for g in range(BODY_GROUPS):
             tile = load_group(Wk_words, g)
-            for j in range(BANKS):
-                multiply(k_acc[j], g, 1, j, tile[:, j, :], g == 0, False)
+            multiply_k(g, 0, N_OUT, tile[:].rearrange("p j n -> p (j n)"))
             if FIRST_TURN_GROUP <= g < FIRST_TURN_GROUP + BANKS:
                 turn_heads(g - FIRST_TURN_GROUP)
-            if FIRST_TURN_GROUP + BANKS <= g < FIRST_TURN_GROUP + 2 * BANKS:
-                turn_runs((g - FIRST_TURN_GROUP - BANKS) * BANK_HEADS)
         tail_tiles = []
-        for j in range(BANKS):
-            tile = weights.tile([P, TAIL_GROUPS, N_BANK], U32, tag="words", align_bytes=64)
-            for i in range(TAIL_GROUPS):
-                block = Wk_words[body + i].rearrange("p n t -> p (n t)")[
-                    :, j * N_BANK * PACK : (j + 1) * N_BANK * PACK
-                ]
-                nc.sync.dma_start(out=tile[:, i, :].bitcast(I32), in_=block.bitcast(I32))
+        for g0, groups, first, cols in TAIL_LOADS:
+            tile = weights.tile([P, groups, cols], U32, tag="words", align_bytes=64)
+            nc.sync.dma_start(
+                out=tile[:].bitcast(I32),
+                in_=Wk_words[g0 : g0 + groups, :, first : first + cols, :]
+                .rearrange("g p n t -> p g (n t)")
+                .bitcast(I32),
+            )
             tail_tiles.append(tile)
 
-        nc.sync.dma_start(
-            out=out_0[0].rearrange("h (b r) f -> (h b) (r f)", r=RUN),
-            in_=q_out[:].rearrange("p r f -> p (r f)"),
-        )
-        k_result = const.tile([P, BANKS, N_BANK], F32)
-        for j in range(BANKS):
-            for i in range(TAIL_GROUPS):
-                multiply(
-                    k_acc[j], body + i, 1, j, tail_tiles[j][:, i, :], False, i == TAIL_GROUPS - 1
+        k_result = const.tile([P, N_OUT], F32)
+        for i, (g0, groups, first, cols) in enumerate(TAIL_LOADS):
+            for g in range(g0, g0 + groups):
+                multiply_k(g, first, cols, tail_tiles[i][:, g - g0, :])
+            if i < BANKS:
+                turn_runs(i * BANK_HEADS)
+            if i == BANKS - 1:
+                nc.sync.dma_start(
+                    out=out_0[0].rearrange("h (b r) f -> (h b) (r f)", r=RUN),
+                    in_=q_out[:].rearrange("p r f -> p (r f)"),
                 )
-            finish(k_acc[j], 1, j, k_result[:, j, :])
-            nc.sync.dma_start(
-                out=out_1[0, j * BANK_HEADS : (j + 1) * BANK_HEADS].rearrange("h p f -> p h f"),
-                in_=k_result[:, j, :].rearrange("p (h f) -> p h f", f=FEATURES),
-            )
+            for col, width in K_BLOCKS:
+                if g0 + groups == GROUPS and first <= col < first + cols:
+                    result = k_result[:, col : col + width]
+                    finish(k_acc[col], 1, col, result)
+                    h0 = col // FEATURES
+                    nc.sync.dma_start(
+                        out=out_1[0, h0 : h0 + width // FEATURES].rearrange("h p f -> p h f"),
+                        in_=result.rearrange("p (h f) -> p h f", f=FEATURES),
+                    )

@@ -129,41 +129,46 @@ def rotation_tables(nc, const, scratch, pos_i, pair_i):
     cos_sin = scratch.tile([P, 2, PAIRS], F32)
     nc.scalar.activation(out=cos_sin[:], in_=wrapped[:], func=ACT.Sin, scale=2.0 * math.pi)
 
-    rot = const.tile([P, 2, 2, PAIRS], F32)
+    rot = const.tile([P, 2, 2, PAIRS, 2], F32)
     for w in range(2):
-        nc.vector.tensor_tensor(
-            out=rot[:, w, :, :],
-            in0=cos_sin[:],
-            in1=xpos_scale[:, w, :].unsqueeze(1).to_broadcast([P, 2, PAIRS]),
-            op=ALU.mult,
+        for e in range(2):
+            nc.vector.tensor_tensor(
+                out=rot[:, w, :, :, e],
+                in0=cos_sin[:],
+                in1=xpos_scale[:, w, :].unsqueeze(1).to_broadcast([P, 2, PAIRS]),
+                op=ALU.mult,
+            )
+        nc.vector.tensor_scalar_mul(
+            out=rot[:, w, 1, :, 1], in0=rot[:, w, 1, :, 1], scalar1=-1.0
         )
-    return rot
+    return rot[:].rearrange("p w c m e -> p w c (m e)")
 
 
-def rotate_bank(nc, work, bank, cos_sin):
-    heads = bank.shape[1] // FEATURES
-    shape = [P, 2, heads, PAIRS]
-    halves = bank.rearrange("p (h m e) -> p e h m", h=heads, e=2)
+def rotate(nc, work, acc, cos_sin, result):
+    heads = result.shape[1] // FEATURES
+    shape = [P, heads, FEATURES]
+    acc = acc.rearrange("p (h f) -> p h f", f=FEATURES)
     by_cos = work.tile(shape, F32)
     nc.vector.tensor_tensor(
         out=by_cos[:],
-        in0=halves,
-        in1=cos_sin[:, 0, :].unsqueeze(1).unsqueeze(1).to_broadcast(shape),
+        in0=acc,
+        in1=cos_sin[:, 0, :].unsqueeze(1).to_broadcast(shape),
         op=ALU.mult,
     )
     by_sin = work.tile(shape, F32)
     nc.vector.tensor_tensor(
         out=by_sin[:],
-        in0=halves,
-        in1=cos_sin[:, 1, :].unsqueeze(1).unsqueeze(1).to_broadcast(shape),
+        in0=acc,
+        in1=cos_sin[:, 1, :].unsqueeze(1).to_broadcast(shape),
         op=ALU.mult,
     )
-    rotated = work.tile(shape, F32)
+    pairs = "p h (m e) -> p (h m) e"
     nc.vector.tensor_tensor(
-        out=rotated[:, 0], in0=by_cos[:, 0], in1=by_sin[:, 1], op=ALU.subtract
+        out=result.rearrange("p (q e) -> p q e", e=2),
+        in0=by_cos[:].rearrange(pairs, e=2),
+        in1=by_sin[:].rearrange(pairs, e=2)[:, :, ::-1],
+        op=ALU.add,
     )
-    nc.vector.tensor_tensor(out=rotated[:, 1], in0=by_cos[:, 1], in1=by_sin[:, 0], op=ALU.add)
-    return rotated
 
 
 def tile_gatedmultiscaleretentionlayer_pa_k_kernel(
@@ -249,11 +254,7 @@ def tile_gatedmultiscaleretentionlayer_pa_k_kernel(
             nc.tensor.matmul(
                 out=spread[:], lhsT=ones[:], rhs=bias_rows[:, w, cols], start=True, stop=True
             )
-            rotated = rotate_bank(nc, work, spread[:], rot[:, w])
-            nc.vector.tensor_copy(
-                out=bias_rot[:, w, cols].rearrange("p (h m e) -> p h m e", h=BANK_HEADS, e=2),
-                in_=rotated[:].rearrange("p e h m -> p h m e"),
-            )
+            rotate(nc, work, spread[:], rot[:, w], bias_rot[:, w, cols])
 
         def multiply(acc, g, w, col, words, start, stop):
             offset = 4 * (g % PLANES)
@@ -269,13 +270,12 @@ def tile_gatedmultiscaleretentionlayer_pa_k_kernel(
 
         def finish(acc, w, col, result):
             width = result.shape[1]
-            rotated = rotate_bank(nc, work, acc[:], rot[:, w])
+            rotated = work.tile([P, width], F32)
+            rotate(nc, work, acc[:], rot[:, w], rotated[:])
             nc.vector.tensor_tensor(
-                out=result.rearrange("p (h m e) -> p h m e", m=PAIRS, e=2),
-                in0=rotated[:].rearrange("p e h m -> p h m e"),
-                in1=bias_rot[:, w, col : col + width].rearrange(
-                    "p (h m e) -> p h m e", m=PAIRS, e=2
-                ),
+                out=result,
+                in0=rotated[:],
+                in1=bias_rot[:, w, col : col + width],
                 op=ALU.add,
             )
 

@@ -30,31 +30,27 @@ PLANES = 4
 QUADRANTS = 4
 QUADRANT = 32
 
+X_LOADS = 2
 X_CHUNKS = 4
 CHUNK_GROUPS = GROUPS // X_CHUNKS
 BANK_GROUPS = 2
 
 K_BLOCKS = ((0, 512), (512, 512), (1024, 512), (1536, 256), (1792, 256))
-BODY_GROUPS = 8
-TAIL_LOADS = (
-    (8, 2, 0, 1024),
-    (10, 2, 0, 1024),
-    (12, 2, 0, 1024),
-    (14, 2, 0, 1024),
-    (8, 2, 1024, 1024),
-    (10, 3, 1024, 512),
-    (13, 3, 1024, 512),
-    (10, 2, 1536, 512),
-    (12, 4, 1536, 256),
-    (12, 4, 1792, 256),
+PAIR_ENDS = (512, 1024, 1792)
+K_LOADS = tuple((g, 1, 0, 1536) for g in range(GROUPS)) + (
+    (0, 4, 1536, 512),
+    (4, 4, 1536, 512),
+    (8, 3, 1536, 512),
+    (11, 5, 1536, 256),
+    (11, 4, 1792, 256),
+    (15, 1, 1792, 256),
 )
+LOADS_AHEAD = 11
 WEIGHT_BUFS = 12
 
 FIRST_BIAS_GROUP = 3
 
-RUNS = P // HEADS
-RUN = P // RUNS
-FIRST_TURN_GROUP = 3
+FIRST_TURN = 3
 
 THETA = 10000.0
 SCALE_BASE = 512.0
@@ -144,29 +140,25 @@ def rotation_tables(nc, const, scratch, pos_i, pair_i):
     return rot[:].rearrange("p w c m e -> p w c (m e)")
 
 
-def rotate(nc, work, acc, cos_sin, result):
-    heads = result.shape[1] // FEATURES
-    shape = [P, heads, FEATURES]
-    acc = acc.rearrange("p (h f) -> p h f", f=FEATURES)
-    by_cos = work.tile(shape, F32)
+def products(nc, work, acc, cos_sin):
+    width = acc.shape[1]
+    shape = [P, 2, width // FEATURES, FEATURES]
+    both = work.tile([P, 2, width], F32)
     nc.vector.tensor_tensor(
-        out=by_cos[:],
-        in0=acc,
-        in1=cos_sin[:, 0, :].unsqueeze(1).to_broadcast(shape),
+        out=both[:].rearrange("p c (h f) -> p c h f", f=FEATURES),
+        in0=acc.rearrange("p (h f) -> p h f", f=FEATURES).unsqueeze(1).to_broadcast(shape),
+        in1=cos_sin.unsqueeze(2).to_broadcast(shape),
         op=ALU.mult,
     )
-    by_sin = work.tile(shape, F32)
+    return both
+
+
+def add_products(nc, both, rotated):
+    pairs = "p (q e) -> p q e"
     nc.vector.tensor_tensor(
-        out=by_sin[:],
-        in0=acc,
-        in1=cos_sin[:, 1, :].unsqueeze(1).to_broadcast(shape),
-        op=ALU.mult,
-    )
-    pairs = "p h (m e) -> p (h m) e"
-    nc.vector.tensor_tensor(
-        out=result.rearrange("p (q e) -> p q e", e=2),
-        in0=by_cos[:].rearrange(pairs, e=2),
-        in1=by_sin[:].rearrange(pairs, e=2)[:, :, ::-1],
+        out=rotated.rearrange(pairs, e=2),
+        in0=both[:, 0, :].rearrange(pairs, e=2),
+        in1=both[:, 1, :].rearrange(pairs, e=2)[:, :, ::-1],
         op=ALU.add,
     )
 
@@ -181,6 +173,7 @@ def tile_gatedmultiscaleretentionlayer_pa_k_kernel(
         tc.tile_pool(name="scratch", bufs=1) as scratch,
         tc.tile_pool(name="weights", bufs=WEIGHT_BUFS) as weights,
         tc.tile_pool(name="work", bufs=2) as work,
+        tc.tile_pool(name="turning", bufs=1) as turning,
         tc.psum_pool(name="psum", bufs=4) as psum,
     ):
         bias_rows = const.tile([P, 2, N_OUT], BF16)
@@ -193,9 +186,9 @@ def tile_gatedmultiscaleretentionlayer_pa_k_kernel(
         nc.vector.memset(ones[:], 1.0)
 
         x_sb = const.tile([P, D], BF16)
-        chunk_cols = D // X_CHUNKS
-        for c in range(X_CHUNKS):
-            cols = slice(c * chunk_cols, (c + 1) * chunk_cols)
+        load_cols = D // X_LOADS
+        for c in range(X_LOADS):
+            cols = slice(c * load_cols, (c + 1) * load_cols)
             nc.sync.dma_start(out=x_sb[:, cols], in_=x[0, :, cols])
         for w, bias in enumerate((bq, bk)):
             nc.sync.dma_start(out=bias_rows[0:1, w, :], in_=bias.unsqueeze(0))
@@ -254,7 +247,8 @@ def tile_gatedmultiscaleretentionlayer_pa_k_kernel(
             nc.tensor.matmul(
                 out=spread[:], lhsT=ones[:], rhs=bias_rows[:, w, cols], start=True, stop=True
             )
-            rotate(nc, work, spread[:], rot[:, w], bias_rot[:, w, cols])
+            both = products(nc, work, spread[:], rot[:, w])
+            add_products(nc, both, bias_rot[:, w, cols])
 
         def multiply(acc, g, w, col, words, start, stop):
             offset = 4 * (g % PLANES)
@@ -268,16 +262,16 @@ def tile_gatedmultiscaleretentionlayer_pa_k_kernel(
                 stop=stop,
             )
 
-        def finish(acc, w, col, result):
-            width = result.shape[1]
-            rotated = work.tile([P, width], F32)
-            rotate(nc, work, acc[:], rot[:, w], rotated[:])
-            nc.vector.tensor_tensor(
-                out=result,
-                in0=rotated[:],
-                in1=bias_rot[:, w, col : col + width],
-                op=ALU.add,
-            )
+        def finish(w, blocks, multiplied):
+            for both, (acc, col, result) in zip(multiplied, blocks):
+                add_products(nc, both, result)
+            for acc, col, result in blocks:
+                nc.vector.tensor_tensor(
+                    out=result,
+                    in0=result,
+                    in1=bias_rot[:, w, col : col + result.shape[1]],
+                    op=ALU.add,
+                )
 
         def load_group(words_dram, g):
             tile = weights.tile([P, BANKS, N_BANK], U32, tag="words", align_bytes=64)
@@ -299,33 +293,38 @@ def tile_gatedmultiscaleretentionlayer_pa_k_kernel(
             if 0 <= b < 2 * BANKS:
                 rotate_bias(b // BANKS, b % BANKS)
         q_result = const.tile([P, BANKS, N_BANK], F32)
-        for j in range(BANKS):
-            finish(q_acc[j], 0, j * N_BANK, q_result[:, j, :])
+        for j in range(0, BANKS, 2):
+            pair = [(q_acc[i], i * N_BANK, q_result[:, i, :]) for i in (j, j + 1)]
+            finish(0, pair, [products(nc, work, acc[:], rot[:, 0]) for acc, col, result in pair])
 
-        q_turned = const.tile([P, RUN, HEADS, RUNS], F32)
-        q_out = const.tile([P, RUN, FEATURES], F32)
-
-        def turn_heads(j):
-            turned = psum.tile([P, BANK_HEADS, P], F32, tag="q_bank", bufs=3)
+        def turn_heads(result, turned, h0):
+            bank = psum.tile([P, BANK_HEADS, P], F32, tag="q_bank", bufs=3)
             for i in range(BANK_HEADS):
-                cols = slice(i * FEATURES, (i + 1) * FEATURES)
-                nc.tensor.transpose(
-                    out=turned[:, i, :], in_=q_result[:, j, cols], identity=ident[:]
-                )
+                cols = slice((h0 + i) * FEATURES, (h0 + i + 1) * FEATURES)
+                nc.tensor.transpose(out=bank[:, i, :], in_=result[:, cols], identity=ident[:])
             nc.scalar.copy(
-                out=q_turned[:, :, j * BANK_HEADS : (j + 1) * BANK_HEADS, :],
-                in_=turned[:].rearrange("f h (b r) -> f r h b", r=RUN),
+                out=turned[:, :, h0 : h0 + BANK_HEADS, :],
+                in_=bank[:].rearrange("f h (b r) -> f r h b", r=turned.shape[1]),
             )
 
-        def turn_runs(r0):
-            turned = psum.tile([P, BANK_HEADS, FEATURES], F32, tag="q_bank", bufs=3)
+        def turn_runs(turned, runs, r0):
+            bank = psum.tile([P, BANK_HEADS, FEATURES], F32, tag="q_bank", bufs=3)
             for i in range(BANK_HEADS):
                 nc.tensor.transpose(
-                    out=turned[:, i, :],
-                    in_=q_turned[:, r0 + i, :, :].rearrange("f h b -> f (h b)"),
+                    out=bank[:, i, :],
+                    in_=turned[:, r0 + i, :, :].rearrange("f h b -> f (h b)"),
                     identity=ident[:],
                 )
-            nc.scalar.copy(out=q_out[:, r0 : r0 + BANK_HEADS, :], in_=turned[:])
+            nc.scalar.copy(out=runs[:, r0 : r0 + BANK_HEADS, :], in_=bank[:])
+
+        def store_runs(out, runs):
+            nc.sync.dma_start(
+                out=out.rearrange("h (b r) f -> (h b) (r f)", r=runs.shape[1]),
+                in_=runs[:].rearrange("p r f -> p (r f)"),
+            )
+
+        q_turned = turning.tile([P, HEADS, HEADS, P // HEADS], F32, tag="turned")
+        q_runs = const.tile([P, HEADS, FEATURES], F32)
 
         k_acc = {}
 
@@ -340,13 +339,9 @@ def tile_gatedmultiscaleretentionlayer_pa_k_kernel(
                     block = words[:, col - first : col - first + width]
                     multiply(k_acc[col], g, 1, col, block, g == 0, g == GROUPS - 1)
 
-        for g in range(BODY_GROUPS):
-            tile = load_group(Wk_words, g)
-            multiply_k(g, 0, N_OUT, tile[:].rearrange("p j n -> p (j n)"))
-            if FIRST_TURN_GROUP <= g < FIRST_TURN_GROUP + BANKS:
-                turn_heads(g - FIRST_TURN_GROUP)
-        tail_tiles = []
-        for g0, groups, first, cols in TAIL_LOADS:
+        tiles = []
+
+        def load_k(g0, groups, first, cols):
             tile = weights.tile([P, groups, cols], U32, tag="words", align_bytes=64)
             nc.sync.dma_start(
                 out=tile[:].bitcast(I32),
@@ -354,25 +349,36 @@ def tile_gatedmultiscaleretentionlayer_pa_k_kernel(
                 .rearrange("g p n t -> p g (n t)")
                 .bitcast(I32),
             )
-            tail_tiles.append(tile)
+            tiles.append(tile)
 
         k_result = const.tile([P, N_OUT], F32)
-        for i, (g0, groups, first, cols) in enumerate(TAIL_LOADS):
+        blocks, multiplied = [], []
+        for i, (g0, groups, first, cols) in enumerate(K_LOADS):
+            for load in K_LOADS[len(tiles) : i + 1 + LOADS_AHEAD]:
+                load_k(*load)
             for g in range(g0, g0 + groups):
-                multiply_k(g, first, cols, tail_tiles[i][:, g - g0, :])
-            if i < BANKS:
-                turn_runs(i * BANK_HEADS)
-            if i == BANKS - 1:
-                nc.sync.dma_start(
-                    out=out_0[0].rearrange("h (b r) f -> (h b) (r f)", r=RUN),
-                    in_=q_out[:].rearrange("p r f -> p (r f)"),
+                multiply_k(g, first, cols, tiles[i][:, g - g0, :])
+            turn = i - FIRST_TURN
+            if 0 <= turn < BANKS:
+                turn_heads(
+                    q_result[:].rearrange("p j n -> p (j n)"), q_turned, turn * BANK_HEADS
                 )
+            elif BANKS <= turn < 2 * BANKS:
+                turn_runs(q_turned, q_runs, (turn - BANKS) * BANK_HEADS)
+            if i == GROUPS - 1:
+                store_runs(out_0[0], q_runs)
             for col, width in K_BLOCKS:
                 if g0 + groups == GROUPS and first <= col < first + cols:
-                    result = k_result[:, col : col + width]
-                    finish(k_acc[col], 1, col, result)
-                    h0 = col // FEATURES
-                    nc.sync.dma_start(
-                        out=out_1[0, h0 : h0 + width // FEATURES].rearrange("h p f -> p h f"),
-                        in_=result.rearrange("p (h f) -> p h f", f=FEATURES),
-                    )
+                    acc = k_acc[col]
+                    blocks.append((acc, col, k_result[:, col : col + width]))
+                    multiplied.append(products(nc, work, acc[:], rot[:, 1]))
+                    if col in PAIR_ENDS:
+                        finish(1, blocks, multiplied)
+                        for acc, done, result in blocks:
+                            h0 = done // FEATURES
+                            heads = result.shape[1] // FEATURES
+                            nc.sync.dma_start(
+                                out=out_1[0, h0 : h0 + heads].rearrange("h p f -> p h f"),
+                                in_=result.rearrange("p (h f) -> p h f", f=FEATURES),
+                            )
+                        blocks, multiplied = [], []

import math

import concourse.mybir as mybir
from concourse.masks import make_identity

F32 = mybir.dt.float32
BF16 = mybir.dt.bfloat16
I32 = mybir.dt.int32
U32 = mybir.dt.uint32
U8 = mybir.dt.uint8
FP8X4 = mybir.dt.float8_e4m3fn_x4
ALU = mybir.AluOpType
ACT = mybir.ActivationFunctionType

P = 128
D = 8192
PACK = 4
K_PASS = P * PACK
GROUPS = D // K_PASS
HEADS = 16
FEATURES = 128
PAIRS = FEATURES // 2
N_OUT = HEADS * FEATURES
N_BANK = 512
BANKS = N_OUT // N_BANK
BANK_HEADS = N_BANK // FEATURES
BANK_PAIRS = N_BANK // 2

PLANES = 4
QUADRANTS = 4
QUADRANT = 32

X_LOADS = 2
X_CHUNKS = 4
CHUNK_GROUPS = GROUPS // X_CHUNKS
BANK_GROUPS = 2

K_BLOCKS = ((0, 512), (512, 512), (1024, 512), (1536, 256), (1792, 256))
PAIR_ENDS = (512, 1024, 1792)
K_LOADS = tuple((g, 1, 0, 1536) for g in range(GROUPS)) + (
    (0, 4, 1536, 512),
    (4, 4, 1536, 512),
    (8, 3, 1536, 512),
    (11, 5, 1536, 256),
    (11, 4, 1792, 256),
    (15, 1, 1792, 256),
)
LOADS_AHEAD = 11
WEIGHT_BUFS = 12

FIRST_BIAS_GROUP = 3

FIRST_TURN = 3

THETA = 10000.0
SCALE_BASE = 512.0

FLOPS = 2 * P * D * 2 * N_OUT


def index_tiles(nc, scratch):
    pos_i = scratch.tile([P, 1], I32)
    nc.gpsimd.iota(pos_i[:], pattern=[[0, 1]], base=0, channel_multiplier=1)
    pair_i = scratch.tile([P, PAIRS], I32)
    nc.gpsimd.iota(pair_i[:], pattern=[[1, PAIRS]], base=0, channel_multiplier=0)
    return pos_i, pair_i


def rotation_tables(nc, const, scratch, pos_i, pair_i):
    pos = scratch.tile([P, 1], F32)
    nc.vector.tensor_copy(out=pos[:], in_=pos_i[:])
    pair = scratch.tile([P, PAIRS], F32)
    nc.vector.tensor_copy(out=pair[:], in_=pair_i[:])

    base = scratch.tile([P, PAIRS], F32)
    nc.vector.tensor_scalar(
        out=base[:],
        in0=pair[:],
        scalar1=2.0 / (1.4 * FEATURES),
        scalar2=0.4 / 1.4,
        op0=ALU.mult,
        op1=ALU.add,
    )
    power = scratch.tile([P, 1], F32)
    nc.vector.tensor_scalar(
        out=power[:],
        in0=pos[:],
        scalar1=-float(P // 2),
        scalar2=1.0 / SCALE_BASE,
        op0=ALU.add,
        op1=ALU.mult,
    )
    ln_base = scratch.tile([P, PAIRS], F32)
    nc.scalar.activation(out=ln_base[:], in_=base[:], func=ACT.Ln)
    exponent = scratch.tile([P, 2, PAIRS], F32)
    nc.vector.tensor_scalar_mul(out=exponent[:, 0, :], in0=ln_base[:], scalar1=power[:, 0:1])
    nc.vector.tensor_scalar_mul(out=exponent[:, 1, :], in0=exponent[:, 0, :], scalar1=-1.0)

    freq = scratch.tile([P, PAIRS], F32)
    nc.scalar.activation(out=freq[:], in_=pair[:], func=ACT.Exp, scale=-math.log(THETA) / PAIRS)
    xpos_scale = scratch.tile([P, 2, PAIRS], F32)
    nc.scalar.activation(out=xpos_scale[:], in_=exponent[:], func=ACT.Exp)

    turns = scratch.tile([P, 2, PAIRS], F32)
    nc.vector.tensor_scalar(
        out=turns[:, 1, :],
        in0=freq[:],
        scalar1=pos[:, 0:1],
        scalar2=1.0 / (2.0 * math.pi),
        op0=ALU.mult,
        op1=ALU.mult,
    )
    nc.vector.tensor_scalar_add(out=turns[:, 0, :], in0=turns[:, 1, :], scalar1=0.25)

    whole_i = scratch.tile([P, 2, PAIRS], I32)
    nc.vector.tensor_copy(out=whole_i[:], in_=turns[:])
    whole = scratch.tile([P, 2, PAIRS], F32)
    nc.vector.tensor_copy(out=whole[:], in_=whole_i[:])
    part = scratch.tile([P, 2, PAIRS], F32)
    nc.vector.tensor_tensor(out=part[:], in0=turns[:], in1=whole[:], op=ALU.subtract)
    above = scratch.tile([P, 2, PAIRS], F32)
    nc.vector.tensor_single_scalar(out=above[:], in_=part[:], scalar=0.5, op=ALU.is_gt)
    wrapped = scratch.tile([P, 2, PAIRS], F32)
    nc.vector.tensor_tensor(out=wrapped[:], in0=part[:], in1=above[:], op=ALU.subtract)
    cos_sin = scratch.tile([P, 2, PAIRS], F32)
    nc.scalar.activation(out=cos_sin[:], in_=wrapped[:], func=ACT.Sin, scale=2.0 * math.pi)

    rot = const.tile([P, 2, 2, PAIRS, 2], F32)
    for w in range(2):
        for e in range(2):
            nc.vector.tensor_tensor(
                out=rot[:, w, :, :, e],
                in0=cos_sin[:],
                in1=xpos_scale[:, w, :].unsqueeze(1).to_broadcast([P, 2, PAIRS]),
                op=ALU.mult,
            )
        nc.vector.tensor_scalar_mul(
            out=rot[:, w, 1, :, 1], in0=rot[:, w, 1, :, 1], scalar1=-1.0
        )
    return rot[:].rearrange("p w c m e -> p w c (m e)")


def products(nc, work, acc, cos_sin):
    width = acc.shape[1]
    shape = [P, 2, width // FEATURES, FEATURES]
    both = work.tile([P, 2, width], F32)
    nc.vector.tensor_tensor(
        out=both[:].rearrange("p c (h f) -> p c h f", f=FEATURES),
        in0=acc.rearrange("p (h f) -> p h f", f=FEATURES).unsqueeze(1).to_broadcast(shape),
        in1=cos_sin.unsqueeze(2).to_broadcast(shape),
        op=ALU.mult,
    )
    return both


def add_products(nc, both, rotated):
    pairs = "p (q e) -> p q e"
    nc.vector.tensor_tensor(
        out=rotated.rearrange(pairs, e=2),
        in0=both[:, 0, :].rearrange(pairs, e=2),
        in1=both[:, 1, :].rearrange(pairs, e=2)[:, :, ::-1],
        op=ALU.add,
    )


def tile_gatedmultiscaleretentionlayer_pa_k_kernel(
    tc, x, Wq_words, Wq_scales, bq, Wk_words, Wk_scales, bk, out_0, out_1
):
    nc = tc.nc
    with (
        tc.manual_schedule(),
        tc.tile_pool(name="const", bufs=1) as const,
        tc.tile_pool(name="scratch", bufs=1) as scratch,
        tc.tile_pool(name="weights", bufs=WEIGHT_BUFS) as weights,
        tc.tile_pool(name="work", bufs=2) as work,
        tc.tile_pool(name="turning", bufs=1) as turning,
        tc.psum_pool(name="psum", bufs=4) as psum,
    ):
        bias_rows = const.tile([P, 2, N_OUT], BF16)
        nc.vector.memset(bias_rows[:].bitcast(I32), 0)
        w_planes = const.tile([P, 2, GROUPS // PLANES, N_OUT], U8, align_bytes=64)
        for w in range(2):
            for a in range(GROUPS // PLANES):
                nc.vector.memset(w_planes[:, w, a, :].bitcast(I32), 0)
        ones = const.tile([P, P], BF16)
        nc.vector.memset(ones[:], 1.0)

        x_sb = const.tile([P, D], BF16)
        load_cols = D // X_LOADS
        for c in range(X_LOADS):
            cols = slice(c * load_cols, (c + 1) * load_cols)
            nc.sync.dma_start(out=x_sb[:, cols], in_=x[0, :, cols])
        for w, bias in enumerate((bq, bk)):
            nc.sync.dma_start(out=bias_rows[0:1, w, :], in_=bias.unsqueeze(0))

        ident = const.tile([P, P], F32)
        make_identity(nc, ident[:])
        pos_i, pair_i = index_tiles(nc, scratch)

        for w, scales in enumerate((Wq_scales, Wk_scales)):
            for a in range(GROUPS // PLANES):
                for quadrant in range(QUADRANTS):
                    first = QUADRANT * quadrant
                    nc.gpsimd.dma_start(
                        out=w_planes[first : first + PLANES * 4, w, a, :].bitcast(F32),
                        in_=scales[
                            PLANES * a : PLANES * (a + 1), 4 * quadrant : 4 * (quadrant + 1), :
                        ].bitcast(F32),
                    )

        x_words = x_sb[:].bitcast(F32)
        group_words = K_PASS // 2
        grouped = const.tile([P, GROUPS, P, PACK], BF16, align_bytes=64)
        grouped_words = grouped[:].bitcast(F32)
        x_codes = const.tile([P, GROUPS, P], U32, align_bytes=64)
        x_planes = const.tile([P, GROUPS, P], U8, align_bytes=64)
        for c in range(X_CHUNKS):
            for half in range(CHUNK_GROUPS // BANK_GROUPS):
                g0 = c * CHUNK_GROUPS + half * BANK_GROUPS
                xt = psum.tile([P, BANK_GROUPS, 2, P], F32, tag="x_bank")
                for i in range(BANK_GROUPS):
                    for u in range(2):
                        first = (g0 + i) * group_words + u
                        nc.tensor.transpose(
                            out=xt[:, i, u, :],
                            in_=x_words[:, first : (g0 + i + 1) * group_words : 2],
                            identity=ident[:],
                        )
                copy = nc.vector.tensor_copy if half % 2 == 0 else nc.scalar.copy
                copy(
                    out=grouped_words[:, g0 : g0 + BANK_GROUPS, :, :],
                    in_=xt[:].rearrange("p g u r -> p g r u"),
                )
            gs = slice(c * CHUNK_GROUPS, (c + 1) * CHUNK_GROUPS)
            nc.vector.quantize_mx(
                out=x_codes[:, gs, :].rearrange("p g r -> p (g r)").bitcast(FP8X4),
                scales=x_planes[:, gs, :].rearrange("p g r -> p (g r)"),
                in_=grouped[:, gs, :, :].rearrange("p g r t -> p (g r t)"),
            )

        rot = rotation_tables(nc, const, scratch, pos_i, pair_i)
        bias_rot = const.tile([P, 2, N_OUT], F32)

        def rotate_bias(w, j):
            cols = slice(j * N_BANK, (j + 1) * N_BANK)
            spread = psum.tile([P, N_BANK], F32, tag="x_bank")
            nc.tensor.matmul(
                out=spread[:], lhsT=ones[:], rhs=bias_rows[:, w, cols], start=True, stop=True
            )
            both = products(nc, work, spread[:], rot[:, w])
            add_products(nc, both, bias_rot[:, w, cols])

        def multiply(acc, g, w, col, words, start, stop):
            offset = 4 * (g % PLANES)
            nc.tensor.matmul_mx(
                out=acc[:],
                lhsT=x_codes[:, g, :].bitcast(FP8X4),
                lhsT_scale=x_planes[:, g, :],
                rhs=words.bitcast(FP8X4),
                rhs_scale=w_planes[offset:P, w, g // PLANES, col : col + words.shape[1]],
                start=start,
                stop=stop,
            )

        def finish(w, blocks, multiplied):
            for both, (acc, col, result) in zip(multiplied, blocks):
                add_products(nc, both, result)
            for acc, col, result in blocks:
                nc.vector.tensor_tensor(
                    out=result,
                    in0=result,
                    in1=bias_rot[:, w, col : col + result.shape[1]],
                    op=ALU.add,
                )

        def load_group(words_dram, g):
            tile = weights.tile([P, BANKS, N_BANK], U32, tag="words", align_bytes=64)
            nc.sync.dma_start(
                out=tile[:].rearrange("p j n -> p (j n)").bitcast(I32),
                in_=words_dram[g].rearrange("p n t -> p (n t)").bitcast(I32),
            )
            return tile

        q_acc = []
        for j in range(BANKS):
            tag, bufs = ("last_bank", 1) if j == 0 else ("q_bank", 3)
            q_acc.append(psum.tile([P, N_BANK], F32, tag=tag, bufs=bufs, name="q_acc%d" % j))
        for g in range(GROUPS):
            tile = load_group(Wq_words, g)
            for j in range(BANKS):
                multiply(q_acc[j], g, 0, j * N_BANK, tile[:, j, :], g == 0, g == GROUPS - 1)
            b = g - FIRST_BIAS_GROUP
            if 0 <= b < 2 * BANKS:
                rotate_bias(b // BANKS, b % BANKS)
        q_result = const.tile([P, BANKS, N_BANK], F32)
        for j in range(0, BANKS, 2):
            pair = [(q_acc[i], i * N_BANK, q_result[:, i, :]) for i in (j, j + 1)]
            finish(0, pair, [products(nc, work, acc[:], rot[:, 0]) for acc, col, result in pair])

        def turn_heads(result, turned, h0):
            bank = psum.tile([P, BANK_HEADS, P], F32, tag="q_bank", bufs=3)
            for i in range(BANK_HEADS):
                cols = slice((h0 + i) * FEATURES, (h0 + i + 1) * FEATURES)
                nc.tensor.transpose(out=bank[:, i, :], in_=result[:, cols], identity=ident[:])
            nc.scalar.copy(
                out=turned[:, :, h0 : h0 + BANK_HEADS, :],
                in_=bank[:].rearrange("f h (b r) -> f r h b", r=turned.shape[1]),
            )

        def turn_runs(turned, runs, r0):
            bank = psum.tile([P, BANK_HEADS, FEATURES], F32, tag="q_bank", bufs=3)
            for i in range(BANK_HEADS):
                nc.tensor.transpose(
                    out=bank[:, i, :],
                    in_=turned[:, r0 + i, :, :].rearrange("f h b -> f (h b)"),
                    identity=ident[:],
                )
            nc.scalar.copy(out=runs[:, r0 : r0 + BANK_HEADS, :], in_=bank[:])

        def store_runs(out, runs):
            nc.sync.dma_start(
                out=out.rearrange("h (b r) f -> (h b) (r f)", r=runs.shape[1]),
                in_=runs[:].rearrange("p r f -> p (r f)"),
            )

        q_turned = turning.tile([P, HEADS, HEADS, P // HEADS], F32, tag="turned")
        q_runs = const.tile([P, HEADS, FEATURES], F32)

        k_acc = {}

        def multiply_k(g, first, cols, words):
            for col, width in K_BLOCKS:
                if first <= col < first + cols:
                    if col not in k_acc:
                        tag, bufs = ("x_bank", 4) if len(k_acc) < 4 else ("last_bank", 1)
                        k_acc[col] = psum.tile(
                            [P, width], F32, tag=tag, bufs=bufs, name="k_acc%d" % col
                        )
                    block = words[:, col - first : col - first + width]
                    multiply(k_acc[col], g, 1, col, block, g == 0, g == GROUPS - 1)

        tiles = []

        def load_k(g0, groups, first, cols):
            tile = weights.tile([P, groups, cols], U32, tag="words", align_bytes=64)
            nc.sync.dma_start(
                out=tile[:].bitcast(I32),
                in_=Wk_words[g0 : g0 + groups, :, first : first + cols, :]
                .rearrange("g p n t -> p g (n t)")
                .bitcast(I32),
            )
            tiles.append(tile)

        k_result = const.tile([P, N_OUT], F32)
        blocks, multiplied = [], []
        for i, (g0, groups, first, cols) in enumerate(K_LOADS):
            for load in K_LOADS[len(tiles) : i + 1 + LOADS_AHEAD]:
                load_k(*load)
            for g in range(g0, g0 + groups):
                multiply_k(g, first, cols, tiles[i][:, g - g0, :])
            turn = i - FIRST_TURN
            if 0 <= turn < BANKS:
                turn_heads(
                    q_result[:].rearrange("p j n -> p (j n)"), q_turned, turn * BANK_HEADS
                )
            elif BANKS <= turn < 2 * BANKS:
                turn_runs(q_turned, q_runs, (turn - BANKS) * BANK_HEADS)
            if i == GROUPS - 1:
                store_runs(out_0[0], q_runs)
            for col, width in K_BLOCKS:
                if g0 + groups == GROUPS and first <= col < first + cols:
                    acc = k_acc[col]
                    blocks.append((acc, col, k_result[:, col : col + width]))
                    multiplied.append(products(nc, work, acc[:], rot[:, 1]))
                    if col in PAIR_ENDS:
                        finish(1, blocks, multiplied)
                        for acc, done, result in blocks:
                            h0 = done // FEATURES
                            heads = result.shape[1] // FEATURES
                            nc.sync.dma_start(
                                out=out_1[0, h0 : h0 + heads].rearrange("h p f -> p h f"),
                                in_=result.rearrange("p (h f) -> p h f", f=FEATURES),
                            )
                        blocks, multiplied = [], []
